import numpy as np
import ml_dtypes


def mxq(x, axis, fmt="e4m3"):
    dtype, down = {"e4m3": (ml_dtypes.float8_e4m3fn, 7), "e5m2": (ml_dtypes.float8_e5m2, 14)}[fmt]
    v = np.moveaxis(np.asarray(x, np.float32).astype(ml_dtypes.bfloat16).astype(np.float64), axis, -1)
    blocks = v.reshape(v.shape[:-1] + (-1, 32))
    amax = np.abs(blocks).max(-1, keepdims=True)
    byte = np.maximum(np.where(amax > 0, np.frexp(amax)[1] - 1 + 127, 0) - down, 1)
    scale = np.exp2(byte - 127.0)
    codes = (blocks / scale).astype(np.float32).astype(dtype).astype(np.float64)
    return np.moveaxis((codes * scale).reshape(v.shape), -1, axis)


WIDE = False


def mx_kscale(k):
    if not WIDE:
        return np.ones(k)
    levels = np.array([10, -10, 5, -5, 0])
    a = np.random.permutation(np.resize(levels, k // 512 * 4)).reshape(k // 512, 4)
    idx = np.arange(k)
    return np.exp2(a[idx // 512, idx % 128 // 32])


BF16 = ml_dtypes.bfloat16


def bf(x):
    return np.asarray(x, np.float32).astype(BF16)


def f64(x):
    return np.asarray(x).astype(np.float64)


E2M1 = np.array([0.0, 0.5, 1.0, 1.5, 2.0, 3.0, 4.0, 6.0, -0.0, -0.5, -1.0, -1.5, -2.0, -3.0, -4.0, -6.0])


def pack_weight(w, fmt):
    k, n = w.shape
    w = f64(bf(w)).reshape(k // 32, 32, n)
    amax = np.abs(w).max(1)
    if fmt == "e4m3":
        byte = np.frexp(amax)[1] - 1 + 127 - 7
    else:
        mant, ex = np.frexp(amax / 6.0)
        byte = np.where(mant > 0.5, ex, ex - 1) + 127
    byte = np.clip(np.where(amax > 0, byte, 1), 1, 254)
    scaled = (w * np.exp2(127.0 - byte)[:, None, :]).reshape(k, n).astype(np.float32)
    by_word = np.ascontiguousarray(scaled.reshape(k // 512, 128, 4, n).transpose(0, 1, 3, 2))
    if fmt == "e4m3":
        words = by_word.astype(ml_dtypes.float8_e4m3fn).view(np.uint8)
    else:
        c = by_word.astype(ml_dtypes.float4_e2m1fn).view(np.uint8) & 0xF
        words = c[..., 0::2] | (c[..., 1::2] << 4)
    return np.ascontiguousarray(words), np.ascontiguousarray(byte.astype(np.uint8).reshape(k // 512, 16, n))


def unpack_weight(words, scales, fmt):
    g, p, n, _ = words.shape
    if fmt == "e4m3":
        vals = np.ascontiguousarray(words).view(ml_dtypes.float8_e4m3fn).astype(np.float64)
    else:
        nib = np.empty((g, p, n, 4), np.uint8)
        nib[..., 0::2] = words & 0xF
        nib[..., 1::2] = words >> 4
        vals = E2M1[nib]
    vals = vals * np.repeat(np.exp2(scales.astype(np.float64) - 127.0), 8, axis=1)[..., None]
    return vals.transpose(0, 1, 3, 2).reshape(g * 512, n)

def pack4(w):
    words, scales = pack_weight(w, "e2m1")
    return words.reshape(words.shape[0], 128, -1), scales


def unpack4(words, scales):
    return unpack_weight(words.reshape(words.shape[0], 128, -1, 2), scales, "e2m1")


B, L, N, HID, H, D = 1, 128, 128, 8192, 12, 128


def apply_rope(x, rope):
    xp = x.reshape(x.shape[:-1] + (D // 2, 2))
    rp = rope[:, None].reshape(rope.shape[0], 1, rope.shape[1], D // 2, 2)
    cos, sin = rp[..., 0], rp[..., 1]
    x0, x1 = xp[..., 0], xp[..., 1]
    out = np.stack([x0 * cos - x1 * sin, x1 * cos + x0 * sin], axis=-1)
    return out.reshape(x.shape)


def setup_inputs():
    s = mx_kscale(HID)
    img = bf(np.random.standard_normal((B, N, HID)) * s)
    rope = bf(np.random.standard_normal((B, N, D)))
    w = np.random.standard_normal((3 * H * D, HID)) / np.sqrt(HID) / s
    words, scales = pack4(np.ascontiguousarray(w.T))
    return {"img": img,
            "rope": rope,
            "W_img_qkv_words": words,
            "W_img_qkv_scales": scales}


def reference(img, rope, W_img_qkv_words, W_img_qkv_scales):
    y = mxq(f64(img), 2, "e4m3") @ unpack4(W_img_qkv_words, W_img_qkv_scales)
    y = y.reshape(B, N, 3, H, D).transpose(2, 0, 3, 1, 4)
    r = f64(rope)
    return apply_rope(y[0], r), apply_rope(y[1], r), y[2]

@@ -1,0 +1,222 @@
+from contextlib import ExitStack
+
+import concourse.mybir as mybir
+from concourse.masks import make_identity
+
+F32 = mybir.dt.float32
+BF16 = mybir.dt.bfloat16
+I32 = mybir.dt.int32
+U32 = mybir.dt.uint32
+U8 = mybir.dt.uint8
+FP8X4 = mybir.dt.float8_e4m3fn_x4
+FP4X4 = mybir.dt.float4_e2m1fn_x4
+MULT = mybir.AluOpType.mult
+ADD = mybir.AluOpType.add
+
+P = 128
+K = 8192
+K_PASS = 512
+GROUPS = K // K_PASS
+HEAD = 128
+PAIRS = HEAD // 2
+BANK_COLS = 512
+BANK_HEADS = BANK_COLS // HEAD
+BANK_BYTES = 2 * BANK_COLS
+BANKS = 9
+ROPE_BANKS = 6
+ROUNDS = ((0, 5), (5, 9))
+G_CHUNK = 2
+CHUNKS = GROUPS // G_CHUNK
+G_HALF = GROUPS // 2
+IMG_PIECES = 4
+G_PIECE = GROUPS // IMG_PIECES
+
+FLOPS = 2 * P * K * BANKS * BANK_COLS
+
+
+def tile_jointattention_pa_k_kernel(tc, img, rope, w_words, w_scales, out_q, out_k, out_v):
+    nc = tc.nc
+    outs = (out_q, out_k, out_v)
+    words32 = w_words.bitcast(I32)
+    scales32 = w_scales.bitcast(I32)
+
+    with ExitStack() as ctx:
+        ctx.enter_context(tc.manual_schedule())
+        keep = ctx.enter_context(tc.tile_pool(name="keep", bufs=1))
+        stream = ctx.enter_context(tc.tile_pool(name="stream", bufs=CHUNKS))
+        work = ctx.enter_context(tc.tile_pool(name="work", bufs=2))
+        psum = ctx.enter_context(tc.psum_pool(name="psum", bufs=8))
+
+        planes = {}
+        for r, (first_bank, end_bank) in enumerate(ROUNDS):
+            for half in range(2):
+                planes[(r, half)] = keep.tile(
+                    [P, G_HALF, (end_bank - first_bank) * BANK_COLS],
+                    U8,
+                    name="plane_%d_%d" % (r, half),
+                    align_bytes=64,
+                )
+
+        def zero_planes(r):
+            for half in range(2):
+                flat = planes[(r, half)][:].rearrange("p g n -> p (g n)")
+                nc.vector.memset(flat.bitcast(I32), 0)
+
+        def load_scales(r):
+            first_bank, end_bank = ROUNDS[r]
+            cols = slice(first_bank * BANK_COLS // 4, end_bank * BANK_COLS // 4)
+            for half in range(2):
+                groups = slice(half * G_HALF, (half + 1) * G_HALF)
+                for q in range(8):
+                    partition = 32 * (q // 4) + q % 4
+                    nc.sync.dma_start(
+                        out=planes[(r, half)][partition:P:64, :, :].bitcast(I32),
+                        in_=scales32[groups, q:16:8, cols].rearrange("g q n -> q g n"),
+                    )
+
+        def load_words(r, chunk):
+            first_bank, end_bank = ROUNDS[r]
+            words = stream.tile(
+                [P, G_CHUNK, (end_bank - first_bank) * BANK_BYTES],
+                U8,
+                name="words",
+                tag="words",
+                align_bytes=64,
+            )
+            nc.sync.dma_start(
+                out=words[:].bitcast(I32),
+                in_=words32[
+                    chunk * G_CHUNK : (chunk + 1) * G_CHUNK,
+                    :,
+                    first_bank * BANK_BYTES // 4 : end_bank * BANK_BYTES // 4,
+                ].rearrange("g p n -> p g n"),
+            )
+            return words
+
+        zero_planes(0)
+        identity = keep.tile([P, P], F32, name="identity")
+        make_identity(nc, identity[:])
+
+        img_pieces = []
+        for piece in range(IMG_PIECES):
+            img_sb = keep.tile([P, G_PIECE * K_PASS], BF16, name="img_%d" % piece)
+            nc.sync.dma_start(
+                out=img_sb[:],
+                in_=img[0, :, piece * G_PIECE * K_PASS : (piece + 1) * G_PIECE * K_PASS],
+            )
+            img_pieces.append(img_sb)
+        rope_sb = keep.tile([P, HEAD], BF16, name="rope_sb")
+        nc.scalar.dma_start(out=rope_sb[:], in_=rope[0])
+
+        load_scales(0)
+        round_words = [load_words(0, chunk) for chunk in range(CHUNKS)]
+
+        img_codes = keep.tile([P, GROUPS, P], U32, name="img_codes", align_bytes=64)
+        img_scales = keep.tile([P, GROUPS, P], U8, name="img_scales", align_bytes=64)
+        for piece in range(IMG_PIECES):
+            img_words = img_pieces[piece][:].bitcast(F32)
+            grouped = keep.tile([P, G_PIECE, K_PASS], BF16, name="grouped_%d" % piece, align_bytes=64)
+            grouped_words = grouped[:].bitcast(F32).rearrange("p g (t u) -> p g t u", u=2)
+            for pair in range(G_PIECE // 2):
+                flipped = psum.tile([P, 2, 2, P], F32, name="flipped", tag="bank")
+                for g in range(2):
+                    first_word = (2 * pair + g) * (K_PASS // 2)
+                    for u in range(2):
+                        nc.tensor.transpose(
+                            flipped[:, g, u, :],
+                            img_words[:, first_word + u : first_word + K_PASS // 2 : 2],
+                            identity[:],
+                        )
+                copy = nc.vector.tensor_copy if pair % 2 == 0 else nc.scalar.copy
+                copy(
+                    out=grouped_words[:, 2 * pair : 2 * pair + 2, :, :],
+                    in_=flipped[:].rearrange("p g u t -> p g t u"),
+                )
+            groups = slice(piece * G_PIECE, (piece + 1) * G_PIECE)
+            nc.vector.quantize_mx(
+                out=img_codes[:, groups, :].rearrange("p g t -> p (g t)").bitcast(FP8X4),
+                scales=img_scales[:, groups, :].rearrange("p g t -> p (g t)"),
+                in_=grouped[:].rearrange("p g c -> p (g c)"),
+            )
+
+        rope_pairs = rope_sb[:].rearrange("p (i e) -> p i e", e=2)
+        cos_twice = keep.tile([P, PAIRS, 2], F32, name="cos_twice")
+        nc.vector.tensor_copy(out=cos_twice[:], in_=rope_pairs[:, :, 0:1].to_broadcast([P, PAIRS, 2]))
+        sin_signed = keep.tile([P, 2, PAIRS], F32, name="sin_signed")
+        nc.vector.tensor_scalar_mul(out=sin_signed[:, 0, :], in0=rope_pairs[:, :, 1], scalar1=-1.0)
+        nc.vector.tensor_copy(out=sin_signed[:, 1, :], in_=rope_pairs[:, :, 1])
+
+        zero_planes(1)
+
+        def multiply(r, words_of_chunk):
+            first_bank, end_bank = ROUNDS[r]
+            sums = [
+                psum.tile([P, BANK_COLS], F32, name="sums", tag="bank")
+                for bank in range(first_bank, end_bank)
+            ]
+            for chunk in range(CHUNKS):
+                for j in range(end_bank - first_bank):
+                    for g_in_chunk in range(G_CHUNK):
+                        g = chunk * G_CHUNK + g_in_chunk
+                        nc.tensor.matmul_mx(
+                            out=sums[j][:],
+                            lhsT=img_codes[:, g, :].bitcast(FP8X4),
+                            lhsT_scale=img_scales[:, g, :],
+                            rhs=words_of_chunk[chunk][
+                                :, g_in_chunk, j * BANK_BYTES : (j + 1) * BANK_BYTES
+                            ].bitcast(FP4X4),
+                            rhs_scale=planes[(r, g // G_HALF)][
+                                :, g % G_HALF, j * BANK_COLS : (j + 1) * BANK_COLS
+                            ],
+                            start=(g == 0),
+                            stop=(g == GROUPS - 1),
+                        )
+            return sums
+
+        def finish(bank, bank_sums):
+            result = keep.tile([P, BANK_HEADS, HEAD], F32, name="result_%d" % bank)
+            if bank >= ROPE_BANKS:
+                nc.scalar.copy(out=result[:].rearrange("p h d -> p (h d)"), in_=bank_sums[:])
+                return result
+            with_cos = work.tile([P, BANK_HEADS, HEAD], F32, name="with_cos")
+            nc.vector.tensor_tensor(
+                out=with_cos[:],
+                in0=bank_sums[:].rearrange("p (h d) -> p h d", h=BANK_HEADS),
+                in1=cos_twice[:].rearrange("p i e -> p (i e)").unsqueeze(1).to_broadcast([P, BANK_HEADS, HEAD]),
+                op=MULT,
+            )
+            with_sin = work.tile([P, 2, BANK_HEADS, PAIRS], F32, name="with_sin")
+            by_parity = bank_sums[:].rearrange("p (h i e) -> p e h i", h=BANK_HEADS, e=2)
+            for e in range(2):
+                nc.vector.tensor_tensor(
+                    out=with_sin[:, e, :, :],
+                    in0=by_parity[:, 1 - e, :, :],
+                    in1=sin_signed[:, e, :].unsqueeze(1).to_broadcast([P, BANK_HEADS, PAIRS]),
+                    op=MULT,
+                )
+            nc.vector.tensor_tensor(
+                out=result[:].rearrange("p h (i e) -> p h i e", e=2),
+                in0=with_cos[:].rearrange("p h (i e) -> p h i e", e=2),
+                in1=with_sin[:].rearrange("p e h i -> p h i e"),
+                op=ADD,
+            )
+            return result
+
+        def store(bank, result):
+            first_head = (bank % 3) * BANK_HEADS
+            nc.sync.dma_start(
+                out=outs[bank // 3][0, first_head : first_head + BANK_HEADS, :, :].rearrange("h n d -> n h d"),
+                in_=result[:],
+            )
+
+        first_sums = multiply(0, round_words)
+        first_results = [finish(bank, first_sums[bank]) for bank in range(*ROUNDS[0])]
+
+        load_scales(1)
+        round_words = [load_words(1, chunk) for chunk in range(CHUNKS)]
+        for bank in range(*ROUNDS[0]):
+            store(bank, first_results[bank])
+
+        second_sums = multiply(1, round_words)
+        for j, bank in enumerate(range(*ROUNDS[1])):
+            store(bank, finish(bank, second_sums[j]))

@@ -27,7 +27,7 @@ ROPE_BANKS = 6
 ROUNDS = ((0, 5), (5, 9))
 G_CHUNK = 2
 CHUNKS = GROUPS // G_CHUNK
-G_HALF = GROUPS // 2
+G_PLANES = 4
 IMG_PIECES = 4
 G_PIECE = GROUPS // IMG_PIECES
 
@@ -47,31 +47,24 @@ def tile_jointattention_pa_k_kernel(tc, img, rope, w_words, w_scales, out_q, out
         work = ctx.enter_context(tc.tile_pool(name="work", bufs=2))
         psum = ctx.enter_context(tc.psum_pool(name="psum", bufs=8))
 
-        planes = {}
-        for r, (first_bank, end_bank) in enumerate(ROUNDS):
-            for half in range(2):
-                planes[(r, half)] = keep.tile(
-                    [P, G_HALF, (end_bank - first_bank) * BANK_COLS],
-                    U8,
-                    name="plane_%d_%d" % (r, half),
-                    align_bytes=64,
-                )
+        planes = [
+            keep.tile([P, G_PLANES, BANKS * BANK_COLS], U8, name="planes_%d" % i, align_bytes=64)
+            for i in range(GROUPS // G_PLANES)
+        ]
 
-        def zero_planes(r):
-            for half in range(2):
-                flat = planes[(r, half)][:].rearrange("p g n -> p (g n)")
+        def zero_planes():
+            for tile_of_planes in planes:
+                flat = tile_of_planes[:].rearrange("p g n -> p (g n)")
                 nc.vector.memset(flat.bitcast(I32), 0)
 
-        def load_scales(r):
-            first_bank, end_bank = ROUNDS[r]
-            cols = slice(first_bank * BANK_COLS // 4, end_bank * BANK_COLS // 4)
-            for half in range(2):
-                groups = slice(half * G_HALF, (half + 1) * G_HALF)
+        def load_scales():
+            for i, tile_of_planes in enumerate(planes):
+                groups = slice(i * G_PLANES, (i + 1) * G_PLANES)
                 for q in range(8):
                     partition = 32 * (q // 4) + q % 4
                     nc.sync.dma_start(
-                        out=planes[(r, half)][partition:P:64, :, :].bitcast(I32),
-                        in_=scales32[groups, q:16:8, cols].rearrange("g q n -> q g n"),
+                        out=tile_of_planes[partition:P:64, :, :].bitcast(I32),
+                        in_=scales32[groups, q:16:8, :].rearrange("g q n -> q g n"),
                     )
 
         def load_words(r, chunk):
@@ -93,7 +86,7 @@ def tile_jointattention_pa_k_kernel(tc, img, rope, w_words, w_scales, out_q, out
             )
             return words
 
-        zero_planes(0)
+        zero_planes()
         identity = keep.tile([P, P], F32, name="identity")
         make_identity(nc, identity[:])
 
@@ -108,7 +101,7 @@ def tile_jointattention_pa_k_kernel(tc, img, rope, w_words, w_scales, out_q, out
         rope_sb = keep.tile([P, HEAD], BF16, name="rope_sb")
         nc.scalar.dma_start(out=rope_sb[:], in_=rope[0])
 
-        load_scales(0)
+        load_scales()
         round_words = [load_words(0, chunk) for chunk in range(CHUNKS)]
 
         img_codes = keep.tile([P, GROUPS, P], U32, name="img_codes", align_bytes=64)
@@ -146,8 +139,6 @@ def tile_jointattention_pa_k_kernel(tc, img, rope, w_words, w_scales, out_q, out
         nc.vector.tensor_scalar_mul(out=sin_signed[:, 0, :], in0=rope_pairs[:, :, 1], scalar1=-1.0)
         nc.vector.tensor_copy(out=sin_signed[:, 1, :], in_=rope_pairs[:, :, 1])
 
-        zero_planes(1)
-
         def multiply(r, words_of_chunk):
             first_bank, end_bank = ROUNDS[r]
             sums = [
@@ -165,8 +156,8 @@ def tile_jointattention_pa_k_kernel(tc, img, rope, w_words, w_scales, out_q, out
                             rhs=words_of_chunk[chunk][
                                 :, g_in_chunk, j * BANK_BYTES : (j + 1) * BANK_BYTES
                             ].bitcast(FP4X4),
-                            rhs_scale=planes[(r, g // G_HALF)][
-                                :, g % G_HALF, j * BANK_COLS : (j + 1) * BANK_COLS
+                            rhs_scale=planes[g // G_PLANES][
+                                :, g % G_PLANES, (first_bank + j) * BANK_COLS : (first_bank + j + 1) * BANK_COLS
                             ],
                             start=(g == 0),
                             stop=(g == GROUPS - 1),
@@ -212,7 +203,6 @@ def tile_jointattention_pa_k_kernel(tc, img, rope, w_words, w_scales, out_q, out
         first_sums = multiply(0, round_words)
         first_results = [finish(bank, first_sums[bank]) for bank in range(*ROUNDS[0])]
 
-        load_scales(1)
         round_words = [load_words(1, chunk) for chunk in range(CHUNKS)]
         for bank in range(*ROUNDS[0]):
             store(bank, first_results[bank])

@@ -27,7 +27,7 @@ ROPE_BANKS = 6
 ROUNDS = ((0, 5), (5, 9))
 G_CHUNK = 2
 CHUNKS = GROUPS // G_CHUNK
-G_PLANES = 4
+G_PLANES = 2
 IMG_PIECES = 4
 G_PIECE = GROUPS // IMG_PIECES
 

@@ -24,7 +24,7 @@ BANK_HEADS = BANK_COLS // HEAD
 BANK_BYTES = 2 * BANK_COLS
 BANKS = 9
 ROPE_BANKS = 6
-ROUNDS = ((0, 5), (5, 9))
+ROUNDS = ((0, ROPE_BANKS), (ROPE_BANKS, BANKS))
 G_CHUNK = 2
 CHUNKS = GROUPS // G_CHUNK
 G_PLANES = 2
@@ -43,7 +43,6 @@ def tile_jointattention_pa_k_kernel(tc, img, rope, w_words, w_scales, out_q, out
     with ExitStack() as ctx:
         ctx.enter_context(tc.manual_schedule())
         keep = ctx.enter_context(tc.tile_pool(name="keep", bufs=1))
-        stream = ctx.enter_context(tc.tile_pool(name="stream", bufs=CHUNKS))
         work = ctx.enter_context(tc.tile_pool(name="work", bufs=2))
         psum = ctx.enter_context(tc.psum_pool(name="psum", bufs=8))
 
@@ -89,48 +88,45 @@ def tile_jointattention_pa_k_kernel(tc, img, rope, w_words, w_scales, out_q, out
         zero_planes()
         identity = keep.tile([P, P], F32, name="identity")
         make_identity(nc, identity[:])
-
-        img_pieces = []
-        for piece in range(IMG_PIECES):
-            img_sb = keep.tile([P, G_PIECE * K_PASS], BF16, name="img_%d" % piece)
-            nc.sync.dma_start(
-                out=img_sb[:],
-                in_=img[0, :, piece * G_PIECE * K_PASS : (piece + 1) * G_PIECE * K_PASS],
-            )
-            img_pieces.append(img_sb)
         rope_sb = keep.tile([P, HEAD], BF16, name="rope_sb")
         nc.scalar.dma_start(out=rope_sb[:], in_=rope[0])
 
-        load_scales()
-        round_words = [load_words(0, chunk) for chunk in range(CHUNKS)]
-
         img_codes = keep.tile([P, GROUPS, P], U32, name="img_codes", align_bytes=64)
         img_scales = keep.tile([P, GROUPS, P], U8, name="img_scales", align_bytes=64)
-        for piece in range(IMG_PIECES):
-            img_words = img_pieces[piece][:].bitcast(F32)
-            grouped = keep.tile([P, G_PIECE, K_PASS], BF16, name="grouped_%d" % piece, align_bytes=64)
-            grouped_words = grouped[:].bitcast(F32).rearrange("p g (t u) -> p g t u", u=2)
-            for pair in range(G_PIECE // 2):
-                flipped = psum.tile([P, 2, 2, P], F32, name="flipped", tag="bank")
-                for g in range(2):
-                    first_word = (2 * pair + g) * (K_PASS // 2)
-                    for u in range(2):
-                        nc.tensor.transpose(
-                            flipped[:, g, u, :],
-                            img_words[:, first_word + u : first_word + K_PASS // 2 : 2],
-                            identity[:],
-                        )
-                copy = nc.vector.tensor_copy if pair % 2 == 0 else nc.scalar.copy
-                copy(
-                    out=grouped_words[:, 2 * pair : 2 * pair + 2, :, :],
-                    in_=flipped[:].rearrange("p g u t -> p g t u"),
+        with tc.tile_pool(name="unquantised", bufs=1) as unquantised:
+            img_sb = unquantised.tile([P, K], BF16, name="img_sb")
+            nc.sync.dma_start(out=img_sb[:], in_=img[0])
+            load_scales()
+            img_words = img_sb[:].bitcast(F32)
+            for piece in range(IMG_PIECES):
+                grouped = unquantised.tile(
+                    [P, G_PIECE, K_PASS], BF16, name="grouped_%d" % piece, align_bytes=64
                 )
-            groups = slice(piece * G_PIECE, (piece + 1) * G_PIECE)
-            nc.vector.quantize_mx(
-                out=img_codes[:, groups, :].rearrange("p g t -> p (g t)").bitcast(FP8X4),
-                scales=img_scales[:, groups, :].rearrange("p g t -> p (g t)"),
-                in_=grouped[:].rearrange("p g c -> p (g c)"),
-            )
+                grouped_words = grouped[:].bitcast(F32).rearrange("p g (t u) -> p g t u", u=2)
+                for pair in range(G_PIECE // 2):
+                    flipped = psum.tile([P, 2, 2, P], F32, name="flipped", tag="bank")
+                    for g in range(2):
+                        first_word = (piece * G_PIECE + 2 * pair + g) * (K_PASS // 2)
+                        for u in range(2):
+                            nc.tensor.transpose(
+                                flipped[:, g, u, :],
+                                img_words[:, first_word + u : first_word + K_PASS // 2 : 2],
+                                identity[:],
+                            )
+                    copy = nc.vector.tensor_copy if pair % 2 == 0 else nc.scalar.copy
+                    copy(
+                        out=grouped_words[:, 2 * pair : 2 * pair + 2, :, :],
+                        in_=flipped[:].rearrange("p g u t -> p g t u"),
+                    )
+                groups = slice(piece * G_PIECE, (piece + 1) * G_PIECE)
+                nc.vector.quantize_mx(
+                    out=img_codes[:, groups, :].rearrange("p g t -> p (g t)").bitcast(FP8X4),
+                    scales=img_scales[:, groups, :].rearrange("p g t -> p (g t)"),
+                    in_=grouped[:].rearrange("p g c -> p (g c)"),
+                )
+
+        stream = ctx.enter_context(tc.tile_pool(name="stream", bufs=CHUNKS))
+        round_words = [load_words(0, chunk) for chunk in range(CHUNKS)]
 
         rope_pairs = rope_sb[:].rearrange("p (i e) -> p i e", e=2)
         cos_twice = keep.tile([P, PAIRS, 2], F32, name="cos_twice")

@@ -25,7 +25,7 @@ BANK_BYTES = 2 * BANK_COLS
 BANKS = 9
 ROPE_BANKS = 6
 ROUNDS = ((0, ROPE_BANKS), (ROPE_BANKS, BANKS))
-G_CHUNK = 2
+G_CHUNK = 1
 CHUNKS = GROUPS // G_CHUNK
 G_PLANES = 2
 IMG_PIECES = 4

@@ -47,7 +47,7 @@ def tile_jointattention_pa_k_kernel(tc, img, rope, w_words, w_scales, out_q, out
         psum = ctx.enter_context(tc.psum_pool(name="psum", bufs=8))
 
         planes = [
-            keep.tile([P, G_PLANES, BANKS * BANK_COLS], U8, name="planes_%d" % i, align_bytes=64)
+            keep.tile([P, G_PLANES, BANKS * BANK_COLS], U8, name="planes_%d" % i, align_bytes=256)
             for i in range(GROUPS // G_PLANES)
         ]
 
@@ -73,7 +73,7 @@ def tile_jointattention_pa_k_kernel(tc, img, rope, w_words, w_scales, out_q, out
                 U8,
                 name="words",
                 tag="words",
-                align_bytes=64,
+                align_bytes=256,
             )
             nc.sync.dma_start(
                 out=words[:].bitcast(I32),
@@ -91,16 +91,16 @@ def tile_jointattention_pa_k_kernel(tc, img, rope, w_words, w_scales, out_q, out
         rope_sb = keep.tile([P, HEAD], BF16, name="rope_sb")
         nc.scalar.dma_start(out=rope_sb[:], in_=rope[0])
 
-        img_codes = keep.tile([P, GROUPS, P], U32, name="img_codes", align_bytes=64)
-        img_scales = keep.tile([P, GROUPS, P], U8, name="img_scales", align_bytes=64)
+        img_codes = keep.tile([P, GROUPS, P], U32, name="img_codes", align_bytes=256)
+        img_scales = keep.tile([P, GROUPS, P], U8, name="img_scales", align_bytes=256)
         with tc.tile_pool(name="unquantised", bufs=1) as unquantised:
-            img_sb = unquantised.tile([P, K], BF16, name="img_sb")
+            img_sb = unquantised.tile([P, K], BF16, name="img_sb", align_bytes=256)
             nc.sync.dma_start(out=img_sb[:], in_=img[0])
             load_scales()
             img_words = img_sb[:].bitcast(F32)
             for piece in range(IMG_PIECES):
                 grouped = unquantised.tile(
-                    [P, G_PIECE, K_PASS], BF16, name="grouped_%d" % piece, align_bytes=64
+                    [P, G_PIECE, K_PASS], BF16, name="grouped_%d" % piece, align_bytes=256
                 )
                 grouped_words = grouped[:].bitcast(F32).rearrange("p g (t u) -> p g t u", u=2)
                 for pair in range(G_PIECE // 2):
@@ -161,7 +161,7 @@ def tile_jointattention_pa_k_kernel(tc, img, rope, w_words, w_scales, out_q, out
             return sums
 
         def finish(bank, bank_sums):
-            result = keep.tile([P, BANK_HEADS, HEAD], F32, name="result_%d" % bank)
+            result = keep.tile([P, BANK_HEADS, HEAD], F32, name="result_%d" % bank, align_bytes=256)
             if bank >= ROPE_BANKS:
                 nc.scalar.copy(out=result[:].rearrange("p h d -> p (h d)"), in_=bank_sums[:])
                 return result

@@ -47,7 +47,7 @@ def tile_jointattention_pa_k_kernel(tc, img, rope, w_words, w_scales, out_q, out
         psum = ctx.enter_context(tc.psum_pool(name="psum", bufs=8))
 
         planes = [
-            keep.tile([P, G_PLANES, BANKS * BANK_COLS], U8, name="planes_%d" % i, align_bytes=256)
+            keep.tile([P, G_PLANES, BANKS * BANK_COLS], U8, name="planes_%d" % i, align_bytes=1024)
             for i in range(GROUPS // G_PLANES)
         ]
 
@@ -73,7 +73,7 @@ def tile_jointattention_pa_k_kernel(tc, img, rope, w_words, w_scales, out_q, out
                 U8,
                 name="words",
                 tag="words",
-                align_bytes=256,
+                align_bytes=1024,
             )
             nc.sync.dma_start(
                 out=words[:].bitcast(I32),
@@ -91,16 +91,16 @@ def tile_jointattention_pa_k_kernel(tc, img, rope, w_words, w_scales, out_q, out
         rope_sb = keep.tile([P, HEAD], BF16, name="rope_sb")
         nc.scalar.dma_start(out=rope_sb[:], in_=rope[0])
 
-        img_codes = keep.tile([P, GROUPS, P], U32, name="img_codes", align_bytes=256)
-        img_scales = keep.tile([P, GROUPS, P], U8, name="img_scales", align_bytes=256)
+        img_codes = keep.tile([P, GROUPS, P], U32, name="img_codes", align_bytes=1024)
+        img_scales = keep.tile([P, GROUPS, P], U8, name="img_scales", align_bytes=1024)
         with tc.tile_pool(name="unquantised", bufs=1) as unquantised:
-            img_sb = unquantised.tile([P, K], BF16, name="img_sb", align_bytes=256)
+            img_sb = unquantised.tile([P, K], BF16, name="img_sb", align_bytes=1024)
             nc.sync.dma_start(out=img_sb[:], in_=img[0])
             load_scales()
             img_words = img_sb[:].bitcast(F32)
             for piece in range(IMG_PIECES):
                 grouped = unquantised.tile(
-                    [P, G_PIECE, K_PASS], BF16, name="grouped_%d" % piece, align_bytes=256
+                    [P, G_PIECE, K_PASS], BF16, name="grouped_%d" % piece, align_bytes=1024
                 )
                 grouped_words = grouped[:].bitcast(F32).rearrange("p g (t u) -> p g t u", u=2)
                 for pair in range(G_PIECE // 2):
@@ -161,7 +161,7 @@ def tile_jointattention_pa_k_kernel(tc, img, rope, w_words, w_scales, out_q, out
             return sums
 
         def finish(bank, bank_sums):
-            result = keep.tile([P, BANK_HEADS, HEAD], F32, name="result_%d" % bank, align_bytes=256)
+            result = keep.tile([P, BANK_HEADS, HEAD], F32, name="result_%d" % bank, align_bytes=1024)
             if bank >= ROPE_BANKS:
                 nc.scalar.copy(out=result[:].rearrange("p h d -> p (h d)"), in_=bank_sums[:])
                 return result

@@ -27,9 +27,11 @@ ROPE_BANKS = 6
 ROUNDS = ((0, ROPE_BANKS), (ROPE_BANKS, BANKS))
 G_CHUNK = 1
 CHUNKS = GROUPS // G_CHUNK
-G_PLANES = 2
+PLANE_GROUPS = (4, 4, 4, 2, 2)
 IMG_PIECES = 4
 G_PIECE = GROUPS // IMG_PIECES
+PLANE_STEP = 256
+DUMMIES = (6, 4)
 
 FLOPS = 2 * P * K * BANKS * BANK_COLS
 
@@ -47,9 +49,10 @@ def tile_jointattention_pa_k_kernel(tc, img, rope, w_words, w_scales, out_q, out
         psum = ctx.enter_context(tc.psum_pool(name="psum", bufs=8))
 
         planes = [
-            keep.tile([P, G_PLANES, BANKS * BANK_COLS], U8, name="planes_%d" % i, align_bytes=1024)
-            for i in range(GROUPS // G_PLANES)
+            keep.tile([P, count, BANKS * BANK_COLS], U8, name="planes_%d" % i, align_bytes=1024)
+            for i, count in enumerate(PLANE_GROUPS)
         ]
+        plane_of = [planes[i][:, g, :] for i, count in enumerate(PLANE_GROUPS) for g in range(count)]
 
         def zero_planes():
             for tile_of_planes in planes:
@@ -58,13 +61,16 @@ def tile_jointattention_pa_k_kernel(tc, img, rope, w_words, w_scales, out_q, out
 
         def load_scales():
             for i, tile_of_planes in enumerate(planes):
-                groups = slice(i * G_PLANES, (i + 1) * G_PLANES)
+                first_group = sum(PLANE_GROUPS[:i])
+                groups = slice(first_group, first_group + PLANE_GROUPS[i])
                 for q in range(8):
                     partition = 32 * (q // 4) + q % 4
                     nc.sync.dma_start(
                         out=tile_of_planes[partition:P:64, :, :].bitcast(I32),
                         in_=scales32[groups, q:16:8, :].rearrange("g q n -> q g n"),
                     )
+
+        dummy_operands = [keep.tile([P, P + BANK_COLS], BF16, name="zeros_%d" % i) for i in range(len(DUMMIES))]
 
         def load_words(r, chunk):
             first_bank, end_bank = ROUNDS[r]
@@ -88,11 +94,13 @@ def tile_jointattention_pa_k_kernel(tc, img, rope, w_words, w_scales, out_q, out
         zero_planes()
         identity = keep.tile([P, P], F32, name="identity")
         make_identity(nc, identity[:])
+        for zeros in dummy_operands:
+            nc.gpsimd.memset(zeros[:], 0.0)
         rope_sb = keep.tile([P, HEAD], BF16, name="rope_sb")
         nc.scalar.dma_start(out=rope_sb[:], in_=rope[0])
 
         img_codes = keep.tile([P, GROUPS, P], U32, name="img_codes", align_bytes=1024)
-        img_scales = keep.tile([P, GROUPS, P], U8, name="img_scales", align_bytes=1024)
+        img_scales = keep.tile([P, GROUPS, PLANE_STEP], U8, name="img_scales", align_bytes=1024)
         with tc.tile_pool(name="unquantised", bufs=1) as unquantised:
             img_sb = unquantised.tile([P, K], BF16, name="img_sb", align_bytes=1024)
             nc.sync.dma_start(out=img_sb[:], in_=img[0])
@@ -118,12 +126,20 @@ def tile_jointattention_pa_k_kernel(tc, img, rope, w_words, w_scales, out_q, out
                         out=grouped_words[:, 2 * pair : 2 * pair + 2, :, :],
                         in_=flipped[:].rearrange("p g u t -> p g t u"),
                     )
-                groups = slice(piece * G_PIECE, (piece + 1) * G_PIECE)
-                nc.vector.quantize_mx(
-                    out=img_codes[:, groups, :].rearrange("p g t -> p (g t)").bitcast(FP8X4),
-                    scales=img_scales[:, groups, :].rearrange("p g t -> p (g t)"),
-                    in_=grouped[:].rearrange("p g c -> p (g c)"),
-                )
+                for g in range(G_PIECE):
+                    nc.vector.quantize_mx(
+                        out=img_codes[:, piece * G_PIECE + g, :].bitcast(FP8X4),
+                        scales=img_scales[:, piece * G_PIECE + g, :P],
+                        in_=grouped[:, g, :],
+                    )
+
+        dummy_sums = psum.tile([P, BANK_COLS], F32, name="dummy_sums", tag="bank")
+        for zeros, tile_of_planes, count in zip(dummy_operands, planes[-2:], DUMMIES):
+            nc.vector.tensor_scalar_mul(
+                out=zeros[:, :1], in0=tile_of_planes[:, 0, :4].bitcast(I32), scalar1=0.0
+            )
+            for repeat in range(count):
+                nc.tensor.matmul(out=dummy_sums[:], lhsT=zeros[:, :P], rhs=zeros[:, P:], start=True, stop=True)
 
         stream = ctx.enter_context(tc.tile_pool(name="stream", bufs=CHUNKS))
         round_words = [load_words(0, chunk) for chunk in range(CHUNKS)]
@@ -148,12 +164,12 @@ def tile_jointattention_pa_k_kernel(tc, img, rope, w_words, w_scales, out_q, out
                         nc.tensor.matmul_mx(
                             out=sums[j][:],
                             lhsT=img_codes[:, g, :].bitcast(FP8X4),
-                            lhsT_scale=img_scales[:, g, :],
+                            lhsT_scale=img_scales[:, g, :P],
                             rhs=words_of_chunk[chunk][
                                 :, g_in_chunk, j * BANK_BYTES : (j + 1) * BANK_BYTES
                             ].bitcast(FP4X4),
-                            rhs_scale=planes[g // G_PLANES][
-                                :, g % G_PLANES, (first_bank + j) * BANK_COLS : (first_bank + j + 1) * BANK_COLS
+                            rhs_scale=plane_of[g][
+                                :, (first_bank + j) * BANK_COLS : (first_bank + j + 1) * BANK_COLS
                             ],
                             start=(g == 0),
                             stop=(g == GROUPS - 1),
@@ -163,7 +179,8 @@ def tile_jointattention_pa_k_kernel(tc, img, rope, w_words, w_scales, out_q, out
         def finish(bank, bank_sums):
             result = keep.tile([P, BANK_HEADS, HEAD], F32, name="result_%d" % bank, align_bytes=1024)
             if bank >= ROPE_BANKS:
-                nc.scalar.copy(out=result[:].rearrange("p h d -> p (h d)"), in_=bank_sums[:])
+                copy = nc.vector.tensor_copy if bank % 3 == 1 else nc.scalar.copy
+                copy(out=result[:].rearrange("p h d -> p (h d)"), in_=bank_sums[:])
                 return result
             with_cos = work.tile([P, BANK_HEADS, HEAD], F32, name="with_cos")
             nc.vector.tensor_tensor(

from contextlib import ExitStack

import concourse.mybir as mybir
from concourse.masks import make_identity

F32 = mybir.dt.float32
BF16 = mybir.dt.bfloat16
I32 = mybir.dt.int32
U32 = mybir.dt.uint32
U8 = mybir.dt.uint8
FP8X4 = mybir.dt.float8_e4m3fn_x4
FP4X4 = mybir.dt.float4_e2m1fn_x4
MULT = mybir.AluOpType.mult
ADD = mybir.AluOpType.add

P = 128
K = 8192
K_PASS = 512
GROUPS = K // K_PASS
HEAD = 128
PAIRS = HEAD // 2
BANK_COLS = 512
BANK_HEADS = BANK_COLS // HEAD
BANK_BYTES = 2 * BANK_COLS
BANKS = 9
ROPE_BANKS = 6
ROUNDS = ((0, ROPE_BANKS), (ROPE_BANKS, BANKS))
G_CHUNK = 1
CHUNKS = GROUPS // G_CHUNK
PLANE_GROUPS = (4, 4, 4, 2, 2)
IMG_PIECES = 4
G_PIECE = GROUPS // IMG_PIECES
PLANE_STEP = 256
DUMMIES = (6, 4)

FLOPS = 2 * P * K * BANKS * BANK_COLS


def tile_jointattention_pa_k_kernel(tc, img, rope, w_words, w_scales, out_q, out_k, out_v):
    nc = tc.nc
    outs = (out_q, out_k, out_v)
    words32 = w_words.bitcast(I32)
    scales32 = w_scales.bitcast(I32)

    with ExitStack() as ctx:
        ctx.enter_context(tc.manual_schedule())
        keep = ctx.enter_context(tc.tile_pool(name="keep", bufs=1))
        work = ctx.enter_context(tc.tile_pool(name="work", bufs=2))
        psum = ctx.enter_context(tc.psum_pool(name="psum", bufs=8))

        planes = [
            keep.tile([P, count, BANKS * BANK_COLS], U8, name="planes_%d" % i, align_bytes=1024)
            for i, count in enumerate(PLANE_GROUPS)
        ]
        plane_of = [planes[i][:, g, :] for i, count in enumerate(PLANE_GROUPS) for g in range(count)]

        def zero_planes():
            for tile_of_planes in planes:
                flat = tile_of_planes[:].rearrange("p g n -> p (g n)")
                nc.vector.memset(flat.bitcast(I32), 0)

        def load_scales():
            for i, tile_of_planes in enumerate(planes):
                first_group = sum(PLANE_GROUPS[:i])
                groups = slice(first_group, first_group + PLANE_GROUPS[i])
                for q in range(8):
                    partition = 32 * (q // 4) + q % 4
                    nc.sync.dma_start(
                        out=tile_of_planes[partition:P:64, :, :].bitcast(I32),
                        in_=scales32[groups, q:16:8, :].rearrange("g q n -> q g n"),
                    )

        dummy_operands = [keep.tile([P, P + BANK_COLS], BF16, name="zeros_%d" % i) for i in range(len(DUMMIES))]

        def load_words(r, chunk):
            first_bank, end_bank = ROUNDS[r]
            words = stream.tile(
                [P, G_CHUNK, (end_bank - first_bank) * BANK_BYTES],
                U8,
                name="words",
                tag="words",
                align_bytes=1024,
            )
            nc.sync.dma_start(
                out=words[:].bitcast(I32),
                in_=words32[
                    chunk * G_CHUNK : (chunk + 1) * G_CHUNK,
                    :,
                    first_bank * BANK_BYTES // 4 : end_bank * BANK_BYTES // 4,
                ].rearrange("g p n -> p g n"),
            )
            return words

        zero_planes()
        identity = keep.tile([P, P], F32, name="identity")
        make_identity(nc, identity[:])
        for zeros in dummy_operands:
            nc.gpsimd.memset(zeros[:], 0.0)
        rope_sb = keep.tile([P, HEAD], BF16, name="rope_sb")
        nc.scalar.dma_start(out=rope_sb[:], in_=rope[0])

        img_codes = keep.tile([P, GROUPS, P], U32, name="img_codes", align_bytes=1024)
        img_scales = keep.tile([P, GROUPS, PLANE_STEP], U8, name="img_scales", align_bytes=1024)
        with tc.tile_pool(name="unquantised", bufs=1) as unquantised:
            img_sb = unquantised.tile([P, K], BF16, name="img_sb", align_bytes=1024)
            nc.sync.dma_start(out=img_sb[:], in_=img[0])
            load_scales()
            img_words = img_sb[:].bitcast(F32)
            for piece in range(IMG_PIECES):
                grouped = unquantised.tile(
                    [P, G_PIECE, K_PASS], BF16, name="grouped_%d" % piece, align_bytes=1024
                )
                grouped_words = grouped[:].bitcast(F32).rearrange("p g (t u) -> p g t u", u=2)
                for pair in range(G_PIECE // 2):
                    flipped = psum.tile([P, 2, 2, P], F32, name="flipped", tag="bank")
                    for g in range(2):
                        first_word = (piece * G_PIECE + 2 * pair + g) * (K_PASS // 2)
                        for u in range(2):
                            nc.tensor.transpose(
                                flipped[:, g, u, :],
                                img_words[:, first_word + u : first_word + K_PASS // 2 : 2],
                                identity[:],
                            )
                    copy = nc.vector.tensor_copy if pair % 2 == 0 else nc.scalar.copy
                    copy(
                        out=grouped_words[:, 2 * pair : 2 * pair + 2, :, :],
                        in_=flipped[:].rearrange("p g u t -> p g t u"),
                    )
                for g in range(G_PIECE):
                    nc.vector.quantize_mx(
                        out=img_codes[:, piece * G_PIECE + g, :].bitcast(FP8X4),
                        scales=img_scales[:, piece * G_PIECE + g, :P],
                        in_=grouped[:, g, :],
                    )

        dummy_sums = psum.tile([P, BANK_COLS], F32, name="dummy_sums", tag="bank")
        for zeros, tile_of_planes, count in zip(dummy_operands, planes[-2:], DUMMIES):
            nc.vector.tensor_scalar_mul(
                out=zeros[:, :1], in0=tile_of_planes[:, 0, :4].bitcast(I32), scalar1=0.0
            )
            for repeat in range(count):
                nc.tensor.matmul(out=dummy_sums[:], lhsT=zeros[:, :P], rhs=zeros[:, P:], start=True, stop=True)

        stream = ctx.enter_context(tc.tile_pool(name="stream", bufs=CHUNKS))
        round_words = [load_words(0, chunk) for chunk in range(CHUNKS)]

        rope_pairs = rope_sb[:].rearrange("p (i e) -> p i e", e=2)
        cos_twice = keep.tile([P, PAIRS, 2], F32, name="cos_twice")
        nc.vector.tensor_copy(out=cos_twice[:], in_=rope_pairs[:, :, 0:1].to_broadcast([P, PAIRS, 2]))
        sin_signed = keep.tile([P, 2, PAIRS], F32, name="sin_signed")
        nc.vector.tensor_scalar_mul(out=sin_signed[:, 0, :], in0=rope_pairs[:, :, 1], scalar1=-1.0)
        nc.vector.tensor_copy(out=sin_signed[:, 1, :], in_=rope_pairs[:, :, 1])

        def multiply(r, words_of_chunk):
            first_bank, end_bank = ROUNDS[r]
            sums = [
                psum.tile([P, BANK_COLS], F32, name="sums", tag="bank")
                for bank in range(first_bank, end_bank)
            ]
            for chunk in range(CHUNKS):
                for j in range(end_bank - first_bank):
                    for g_in_chunk in range(G_CHUNK):
                        g = chunk * G_CHUNK + g_in_chunk
                        nc.tensor.matmul_mx(
                            out=sums[j][:],
                            lhsT=img_codes[:, g, :].bitcast(FP8X4),
                            lhsT_scale=img_scales[:, g, :P],
                            rhs=words_of_chunk[chunk][
                                :, g_in_chunk, j * BANK_BYTES : (j + 1) * BANK_BYTES
                            ].bitcast(FP4X4),
                            rhs_scale=plane_of[g][
                                :, (first_bank + j) * BANK_COLS : (first_bank + j + 1) * BANK_COLS
                            ],
                            start=(g == 0),
                            stop=(g == GROUPS - 1),
                        )
            return sums

        def finish(bank, bank_sums):
            result = keep.tile([P, BANK_HEADS, HEAD], F32, name="result_%d" % bank, align_bytes=1024)
            if bank >= ROPE_BANKS:
                copy = nc.vector.tensor_copy if bank % 3 == 1 else nc.scalar.copy
                copy(out=result[:].rearrange("p h d -> p (h d)"), in_=bank_sums[:])
                return result
            with_cos = work.tile([P, BANK_HEADS, HEAD], F32, name="with_cos")
            nc.vector.tensor_tensor(
                out=with_cos[:],
                in0=bank_sums[:].rearrange("p (h d) -> p h d", h=BANK_HEADS),
                in1=cos_twice[:].rearrange("p i e -> p (i e)").unsqueeze(1).to_broadcast([P, BANK_HEADS, HEAD]),
                op=MULT,
            )
            with_sin = work.tile([P, 2, BANK_HEADS, PAIRS], F32, name="with_sin")
            by_parity = bank_sums[:].rearrange("p (h i e) -> p e h i", h=BANK_HEADS, e=2)
            for e in range(2):
                nc.vector.tensor_tensor(
                    out=with_sin[:, e, :, :],
                    in0=by_parity[:, 1 - e, :, :],
                    in1=sin_signed[:, e, :].unsqueeze(1).to_broadcast([P, BANK_HEADS, PAIRS]),
                    op=MULT,
                )
            nc.vector.tensor_tensor(
                out=result[:].rearrange("p h (i e) -> p h i e", e=2),
                in0=with_cos[:].rearrange("p h (i e) -> p h i e", e=2),
                in1=with_sin[:].rearrange("p e h i -> p h i e"),
                op=ADD,
            )
            return result

        def store(bank, result):
            first_head = (bank % 3) * BANK_HEADS
            nc.sync.dma_start(
                out=outs[bank // 3][0, first_head : first_head + BANK_HEADS, :, :].rearrange("h n d -> n h d"),
                in_=result[:],
            )

        first_sums = multiply(0, round_words)
        first_results = [finish(bank, first_sums[bank]) for bank in range(*ROUNDS[0])]

        round_words = [load_words(1, chunk) for chunk in range(CHUNKS)]
        for bank in range(*ROUNDS[0]):
            store(bank, first_results[bank])

        second_sums = multiply(1, round_words)
        for j, bank in enumerate(range(*ROUNDS[1])):
            store(bank, finish(bank, second_sums[j]))
